import numpy as np
import ml_dtypes


def mxq(x, axis, fmt="e4m3"):
    dtype, down = {"e4m3": (ml_dtypes.float8_e4m3fn, 7), "e5m2": (ml_dtypes.float8_e5m2, 14)}[fmt]
    v = np.moveaxis(np.asarray(x, np.float32).astype(ml_dtypes.bfloat16).astype(np.float64), axis, -1)
    blocks = v.reshape(v.shape[:-1] + (-1, 32))
    amax = np.abs(blocks).max(-1, keepdims=True)
    byte = np.maximum(np.where(amax > 0, np.frexp(amax)[1] - 1 + 127, 0) - down, 1)
    scale = np.exp2(byte - 127.0)
    codes = (blocks / scale).astype(np.float32).astype(dtype).astype(np.float64)
    return np.moveaxis((codes * scale).reshape(v.shape), -1, axis)


WIDE = False


def mx_kscale(k):
    if not WIDE:
        return np.ones(k)
    levels = np.array([10, -10, 5, -5, 0])
    if k % 512:
        return np.exp2(np.random.permutation(np.resize(levels, k // 32))).repeat(32)
    a = np.empty((k // 512, 16))
    for p in range(k // 512):
        a[p, :8] = np.random.permutation(np.resize(levels, 8))
        for g in range(8):
            far = levels[np.abs(levels - a[p, g]) >= 10]
            a[p, g + 8] = far[np.random.randint(len(far))]
    return np.exp2(a.ravel()).repeat(32)


BF16 = ml_dtypes.bfloat16


def bf(x):
    return np.asarray(x, np.float32).astype(BF16)


def f64(x):
    return np.asarray(x).astype(np.float64)


B, S, I0, I1, I2, I3, I4, O0, O1, O2, O3, O4, R1, R2, R3, R4 = 4, 2048, 4, 4, 2, 2, 16, 2, 2, 2, 2, 8, 16, 512, 1024, 512
IL, OL = I0 * I1 * I2 * I3, O0 * O1 * O2 * O3
IN, OUT = IL * I4, OL * O4


def setup_inputs():
    s = mx_kscale(R4)
    a = mx_kscale(IN)[::I4]
    return {"x": bf(np.random.standard_normal((B, S, IN)) / np.repeat(a, I4)),
            "t3": bf(np.random.standard_normal((IL, OL, R4)) * s * a[:, None, None]),
            "core4": bf(np.random.standard_normal((R4, I4, O4, 1)) / np.sqrt(R4 * IN) / s[:, None, None, None]),
            "bias": bf(np.random.standard_normal(OUT))}


def reference(x, t3, core4, bias):
    p = f64(bf(mxq(f64(t3).reshape(IL * OL, R4), 1, "e4m3") @ mxq(f64(core4).reshape(R4, I4 * O4), 0, "e4m3")))
    m = p.reshape(IL, OL, I4, O4, 1).transpose(0, 2, 1, 3, 4).reshape(IN, OUT, 1)[:, :, 0]
    y = (mxq(f64(x).reshape(B * S, IN), 1, "e4m3") @ mxq(m, 0, "e4m3")) + f64(bias)
    return y.reshape(B, S, OUT)

@@ -1,0 +1,279 @@
+from contextlib import ExitStack
+
+import concourse.mybir as mybir
+from concourse.masks import make_identity
+
+F32 = mybir.dt.float32
+BF16 = mybir.dt.bfloat16
+U32 = mybir.dt.uint32
+U8 = mybir.dt.uint8
+FP8X4 = mybir.dt.float8_e4m3fn_x4
+ADD = mybir.AluOpType.add
+
+P = 128
+TOKENS = 8192
+K2 = 1024
+OUT = 128
+SUB = 4
+GROUP = P * SUB
+NG = TOKENS // GROUP
+BANK_DT = BF16
+PIECES = {0: 4, 1: 2, 2: 2}
+FIRST_PERMUTED = 3
+
+FLOPS = 2 * 1024 * 512 * 128 + 2 * TOKENS * K2 * OUT
+
+
+def tile_linear2mpo_pb_t_kernel(tc, x, t3, core4, bias, out):
+    nc = tc.nc
+    x_v = x.flatten_outer_dims().rearrange("(g p n) k -> g p n k", p=P, n=SUB)
+    o_v = out.flatten_outer_dims().rearrange("(g p n) c -> g p n c", p=P, n=SUB)
+    t3_v = t3.rearrange("(h b c) o r -> b (c o) h r", h=2, b=4)
+    c4_v = core4.rearrange("(p j) i o z -> p j (i o z)", j=4)
+    bias_v = bias.rearrange("(a n) -> a n", a=1)
+
+    with ExitStack() as ctx:
+        keep = ctx.enter_context(tc.tile_pool(name="keep", bufs=1))
+        xin = ctx.enter_context(tc.tile_pool(name="xin", bufs=12))
+        work = ctx.enter_context(tc.tile_pool(name="work", bufs=3))
+        yout = ctx.enter_context(tc.tile_pool(name="yout", bufs=NG))
+        ps_t = ctx.enter_context(tc.psum_pool(name="ps_t", bufs=6))
+        ps_a = ctx.enter_context(tc.psum_pool(name="ps_a", bufs=2))
+        ctx.enter_context(tc.manual_schedule())
+
+        brow = keep.tile([P, OUT], BF16, name="brow")
+        wide = keep.tile([P, 512], BF16, name="wide")
+        nc.vector.memset(wide[:], 1.0)
+        nc.vector.memset(brow[:], 0.0)
+        ones = wide[:, 0:P]
+        ident = keep.tile([P, P], F32, name="ident")
+        make_identity(nc, ident[:])
+
+        c4_sb = keep.tile([P, 4, 128], BF16, name="c4_sb")
+        nc.scalar.dma_start(out=c4_sb[:], in_=c4_v)
+        nc.scalar.dma_start(out=brow[0:1, :], in_=bias_v)
+
+        t3_sb = keep.tile([P, 4, 2, 512], BF16, name="t3_sb")
+        for b in range(4):
+            nc.sync.dma_start(out=t3_sb[:, b], in_=t3_v[b])
+
+        x_words = {}
+
+        def load_x(i):
+            pieces = PIECES.get(i, 1)
+            per = SUB // pieces
+            for c in range(pieces):
+                x_sb = xin.tile([P, per, K2], BF16, name="x_sb")
+                nc.sync.dma_start(out=x_sb[:], in_=x_v[i][:, c * per : (c + 1) * per, :])
+                xw = x_sb[:].rearrange("p n k -> p (n k)").bitcast(F32)
+                for n in range(per):
+                    x_words[(i, c * per + n)] = xw[:, n * 512 : (n + 1) * 512]
+                if pieces == 1:
+                    x_words[(i, "tail")] = xw[:, 1024:2048]
+
+        for i in range(7):
+            load_x(i)
+
+        def dummy(count):
+            wu = ps_t.tile([P, 512], F32, name="wu", tag="tp")
+            for r in range(count):
+                nc.tensor.matmul(wu[:], lhsT=ones, rhs=wide[:], start=True, stop=True)
+
+        dummy(5)
+
+        bias_t = keep.tile([P, SUB, OUT], F32, name="bias_t")
+
+        c4g = keep.tile([P, 512], BF16, name="c4g", align_bytes=64)
+        nc.scalar.copy(
+            out=c4g[:].rearrange("p (x h j) -> p x h j", x=32, h=4, j=4),
+            in_=c4_sb[:].rearrange("p j (h x) -> p x h j", h=4),
+        )
+        c4c = keep.tile([P, 128], U32, name="c4c", align_bytes=64)
+        c4s = keep.tile([P, 128], U8, name="c4s", align_bytes=64)
+        nc.vector.quantize_mx(out=c4c[:].bitcast(FP8X4), scales=c4s[:], in_=c4g[:])
+
+        t3w = t3_sb[:].rearrange("p b h r -> p (b h r)").bitcast(F32)
+        t3g = keep.tile([P, 4096], BF16, name="t3g", align_bytes=64)
+        t3gw = t3g[:].bitcast(F32).rearrange("q (j b o s) -> q j b o s", j=8, b=4, o=16, s=4)
+        for b in range(4):
+            tp = ps_t.tile([P, 4, P], F32, name="tp", tag="tp")
+            for h in range(2):
+                for u in range(2):
+                    base = (b * 2 + h) * 256
+                    nc.tensor.transpose(tp[:, 2 * h + u, :], t3w[:, base + u : base + 256 : 2], ident[:])
+            src = tp[:].rearrange("q s (j o) -> q j o s", j=8)
+            if b % 2 == 0:
+                nc.scalar.copy(out=t3gw[:, :, b], in_=src)
+            else:
+                nc.vector.tensor_copy(out=t3gw[:, :, b], in_=src)
+            if b == 1:
+                pb = ps_a.tile([P, OUT], F32, name="pb", tag="acc")
+                nc.tensor.matmul(pb[:], lhsT=ones, rhs=brow[:], start=True, stop=True)
+                for n in range(SUB):
+                    nc.scalar.copy(out=bias_t[:, n, :], in_=pb[:])
+            if b % 2 == 1:
+                dummy(1)
+        t3c = keep.tile([P, 1024], U32, name="t3c", align_bytes=64)
+        t3s = keep.tile([P, 1024], U8, name="t3s", align_bytes=64)
+
+        xp_tiles = {}
+        xg_tiles = {}
+        xc_tiles = {}
+        acc_tiles = {}
+
+        def permute(i):
+            xp = work.tile([P, 1024], F32, name="xp")
+            nc.vector.tensor_copy(
+                out=xp[:].rearrange("p (a u q) -> p a u q", a=4, u=2),
+                in_=x_words[(i, "tail")].rearrange("p (a q u) -> p a u q", a=4, u=2),
+            )
+            xp_tiles[i] = xp
+
+        def transposes(i, mid_dummy):
+            xg = work.tile([P, SUB * K2], BF16, name="xg", align_bytes=64)
+            xgw = xg[:].bitcast(F32)
+            for n in range(SUB):
+                tp = ps_t.tile([P, 4, P], F32, name="tp", tag="tp")
+                for g in range(2):
+                    for u in range(2):
+                        if i >= FIRST_PERMUTED and n >= 2:
+                            base = ((n - 2) * 4 + g * 2 + u) * P
+                            src = xp_tiles[i][:, base : base + P]
+                        else:
+                            src = x_words[(i, n)][:, g * 256 + u : (g + 1) * 256 : 2]
+                        nc.tensor.transpose(tp[:, 2 * g + u, :], src, ident[:])
+                nc.scalar.copy(
+                    out=xgw[:, n * 512 : (n + 1) * 512].rearrange("q (g t u) -> q g t u", g=2, u=2),
+                    in_=tp[:].rearrange("q (g u) t -> q g t u", g=2),
+                )
+                if mid_dummy and n == 1:
+                    dummy(1)
+            xg_tiles[i] = xg
+
+        def new_codes(i):
+            xc = work.tile([P, SUB * 256], U32, name="xc", align_bytes=64)
+            xs = work.tile([P, SUB * 256], U8, name="xs", align_bytes=64)
+            xc_tiles[i] = (xc, xs)
+
+        def quant(i, n0, n1):
+            xc, xs = xc_tiles[i]
+            nc.vector.quantize_mx(
+                out=xc[:, n0 * 256 : n1 * 256].bitcast(FP8X4),
+                scales=xs[:, n0 * 256 : n1 * 256],
+                in_=xg_tiles[i][:, n0 * 1024 : n1 * 1024],
+            )
+
+        def mm(i):
+            xc, xs = xc_tiles[i]
+            acc = ps_a.tile([P, SUB, OUT], F32, name="acc", tag="acc")
+            for n in range(SUB):
+                for g in range(2):
+                    cols = slice((n * 2 + g) * 128, (n * 2 + g + 1) * 128)
+                    nc.tensor.matmul_mx(
+                        out=acc[:, n, :],
+                        lhsT=xc[:, cols].bitcast(FP8X4),
+                        lhsT_scale=xs[:, cols],
+                        rhs=mc[:, g * 128 : (g + 1) * 128].bitcast(FP8X4),
+                        rhs_scale=ms[:, g * 128 : (g + 1) * 128],
+                        start=(g == 0),
+                        stop=(g == 1),
+                    )
+            acc_tiles[i] = acc
+
+        def finish(i):
+            y = yout.tile([P, SUB, OUT], F32, name="y")
+            nc.vector.tensor_tensor(out=y[:], in0=acc_tiles[i][:], in1=bias_t[:], op=ADD)
+            nc.sync.dma_start(out=o_v[i], in_=y[:])
+
+        for half in range(2):
+            nc.vector.quantize_mx(
+                out=t3c[:, half * 512 : (half + 1) * 512].bitcast(FP8X4),
+                scales=t3s[:, half * 512 : (half + 1) * 512],
+                in_=t3g[:, half * 2048 : (half + 1) * 2048],
+            )
+        transposes(0, True)
+        for i in range(7, 11):
+            load_x(i)
+
+        mA = keep.tile([P, 1024], BF16, name="mA", align_bytes=64)
+        mAv = mA[:].rearrange("m (x j i) -> m x j i", x=32, j=8, i=4)
+        pms = []
+        for hh in range(2):
+            pm = ps_a.tile([P, 4, 128], BANK_DT, name="pm", tag="acc")
+            for jj in range(4):
+                j = hh * 4 + jj
+                nc.tensor.matmul_mx(
+                    out=pm[:, jj, :],
+                    lhsT=t3c[:, j * 128 : (j + 1) * 128].bitcast(FP8X4),
+                    lhsT_scale=t3s[:, j * 128 : (j + 1) * 128],
+                    rhs=c4c[:].bitcast(FP8X4),
+                    rhs_scale=c4s[:],
+                    start=True,
+                    stop=True,
+                )
+            pms.append(pm)
+        new_codes(0)
+        for n in range(SUB):
+            quant(0, n, n + 1)
+        nc.scalar.copy(out=mAv[:, :, 0:4, :], in_=pms[0][:].rearrange("m j (x i) -> m x j i", i=4))
+        nc.vector.tensor_copy(out=mAv[:, :, 4:8, :], in_=pms[1][:].rearrange("m j (x i) -> m x j i", i=4))
+
+        transposes(1, True)
+        dummy(1)
+        for i in range(11, 13):
+            load_x(i)
+        mB = keep.tile([P, 1024], BF16, name="mB", align_bytes=64)
+        mG = keep.tile([P, 1024], BF16, name="mG", align_bytes=64)
+        mc = keep.tile([P, 256], U32, name="mc", align_bytes=64)
+        ms = keep.tile([P, 256], U8, name="ms", align_bytes=64)
+        nc.vector.transpose(out=mB[:], in_=mA[:])
+        mGv = mG[:].rearrange("p (g a o t) -> p g a o t", g=2, a=16, o=8, t=4)
+        mBv = mB[:].rearrange("p (t o a g) -> p g a o t", t=4, o=8, a=16, g=2)
+        for g in range(2):
+            nc.vector.tensor_copy(out=mGv[:, g], in_=mBv[:, g])
+        nc.vector.quantize_mx(out=mc[:].bitcast(FP8X4), scales=ms[:], in_=mG[:])
+
+        transposes(2, False)
+        for i in range(13, 15):
+            load_x(i)
+        mm(0)
+        new_codes(1)
+        quant(1, 0, 2)
+        quant(1, 2, 4)
+        permute(3)
+
+        transposes(3, False)
+        load_x(15)
+        new_codes(2)
+        quant(2, 0, 2)
+        quant(2, 2, 4)
+        mm(1)
+        finish(0)
+        mm(2)
+        finish(1)
+        permute(4)
+
+        for tick in range(4, NG - 1):
+            transposes(tick, False)
+            new_codes(tick - 1)
+            quant(tick - 1, 0, 2)
+            quant(tick - 1, 2, 4)
+            mm(tick - 1)
+            finish(tick - 2)
+            permute(tick + 1)
+
+        last = NG - 1
+        transposes(last, False)
+        new_codes(last - 1)
+        quant(last - 1, 0, 2)
+        quant(last - 1, 2, 4)
+        new_codes(last)
+        quant(last, 0, 1)
+        finish(last - 2)
+        quant(last, 1, 2)
+        quant(last, 2, 3)
+        quant(last, 3, 4)
+        mm(last - 1)
+        mm(last)
+        finish(last - 1)
+        finish(last)

@@ -74,13 +74,6 @@ def tile_linear2mpo_pb_t_kernel(tc, x, t3, core4, bias, out):
         for i in range(7):
             load_x(i)
 
-        def dummy(count):
-            wu = ps_t.tile([P, 512], F32, name="wu", tag="tp")
-            for r in range(count):
-                nc.tensor.matmul(wu[:], lhsT=ones, rhs=wide[:], start=True, stop=True)
-
-        dummy(5)
-
         bias_t = keep.tile([P, SUB, OUT], F32, name="bias_t")
 
         c4g = keep.tile([P, 512], BF16, name="c4g", align_bytes=64)
@@ -111,8 +104,6 @@ def tile_linear2mpo_pb_t_kernel(tc, x, t3, core4, bias, out):
                 nc.tensor.matmul(pb[:], lhsT=ones, rhs=brow[:], start=True, stop=True)
                 for n in range(SUB):
                     nc.scalar.copy(out=bias_t[:, n, :], in_=pb[:])
-            if b % 2 == 1:
-                dummy(1)
         t3c = keep.tile([P, 1024], U32, name="t3c", align_bytes=64)
         t3s = keep.tile([P, 1024], U8, name="t3s", align_bytes=64)
 
@@ -146,8 +137,6 @@ def tile_linear2mpo_pb_t_kernel(tc, x, t3, core4, bias, out):
                     out=xgw[:, n * 512 : (n + 1) * 512].rearrange("q (g t u) -> q g t u", g=2, u=2),
                     in_=tp[:].rearrange("q (g u) t -> q g t u", g=2),
                 )
-                if mid_dummy and n == 1:
-                    dummy(1)
             xg_tiles[i] = xg
 
         def new_codes(i):
@@ -219,7 +208,6 @@ def tile_linear2mpo_pb_t_kernel(tc, x, t3, core4, bias, out):
         nc.vector.tensor_copy(out=mAv[:, :, 4:8, :], in_=pms[1][:].rearrange("m j (x i) -> m x j i", i=4))
 
         transposes(1, True)
-        dummy(1)
         for i in range(11, 13):
             load_x(i)
         mB = keep.tile([P, 1024], BF16, name="mB", align_bytes=64)

@@ -20,6 +20,8 @@ NG = TOKENS // GROUP
 BANK_DT = BF16
 PIECES = {0: 4, 1: 2, 2: 2}
 FIRST_PERMUTED = 3
+V0, NV = 4, 3
+S0, NS = 7, 1
 
 FLOPS = 2 * 1024 * 512 * 128 + 2 * TOKENS * K2 * OUT
 
@@ -69,7 +71,7 @@ def tile_linear2mpo_pb_t_kernel(tc, x, t3, core4, bias, out):
                 for n in range(per):
                     x_words[(i, c * per + n)] = xw[:, n * 512 : (n + 1) * 512]
                 if pieces == 1:
-                    x_words[(i, "tail")] = xw[:, 1024:2048]
+                    x_words[(i, "all")] = xw
 
         for i in range(7):
             load_x(i)
@@ -108,36 +110,65 @@ def tile_linear2mpo_pb_t_kernel(tc, x, t3, core4, bias, out):
         t3s = keep.tile([P, 1024], U8, name="t3s", align_bytes=64)
 
         xp_tiles = {}
+        late = []
+        y_tiles = {}
+        xq_tiles = {}
         xg_tiles = {}
         xc_tiles = {}
         acc_tiles = {}
 
         def permute(i):
-            xp = work.tile([P, 1024], F32, name="xp")
+            xp = work.tile([P, NV * 256], F32, name="xp")
             nc.vector.tensor_copy(
-                out=xp[:].rearrange("p (a u q) -> p a u q", a=4, u=2),
-                in_=x_words[(i, "tail")].rearrange("p (a q u) -> p a u q", a=4, u=2),
+                out=xp[:].rearrange("p (a u q) -> p u a q", a=NV, u=2),
+                in_=x_words[(i, "all")][:, V0 * 256 : (V0 + NV) * 256].rearrange("p (a q u) -> p u a q", a=NV, u=2),
             )
             xp_tiles[i] = xp
 
-        def transposes(i, mid_dummy):
+        def permute_s(i):
+            if NS == 0 or i >= NG:
+                return
+            xq = work.tile([P, NS * 256], F32, name="xq")
+            nc.scalar.copy(
+                out=xq[:].rearrange("p (a u q) -> p a u q", a=NS, u=2),
+                in_=x_words[(i, "all")][:, S0 * 256 : (S0 + NS) * 256].rearrange("p (a q u) -> p a u q", a=NS, u=2),
+            )
+            xq_tiles[i] = xq
+
+        def transposes(i, mid_dummy, by_vector=()):
             xg = work.tile([P, SUB * K2], BF16, name="xg", align_bytes=64)
             xgw = xg[:].bitcast(F32)
             for n in range(SUB):
                 tp = ps_t.tile([P, 4, P], F32, name="tp", tag="tp")
                 for g in range(2):
                     for u in range(2):
-                        if i >= FIRST_PERMUTED and n >= 2:
-                            base = ((n - 2) * 4 + g * 2 + u) * P
+                        blk = 2 * n + g
+                        if i >= FIRST_PERMUTED and V0 <= blk < V0 + NV:
+                            base = ((blk - V0) * 2 + u) * P
                             src = xp_tiles[i][:, base : base + P]
+                        elif i >= FIRST_PERMUTED and S0 <= blk < S0 + NS:
+                            base = ((blk - S0) * 2 + u) * P
+                            src = xq_tiles[i][:, base : base + P]
                         else:
                             src = x_words[(i, n)][:, g * 256 + u : (g + 1) * 256 : 2]
                         nc.tensor.transpose(tp[:, 2 * g + u, :], src, ident[:])
-                nc.scalar.copy(
-                    out=xgw[:, n * 512 : (n + 1) * 512].rearrange("q (g t u) -> q g t u", g=2, u=2),
-                    in_=tp[:].rearrange("q (g u) t -> q g t u", g=2),
-                )
+                if n in by_vector:
+                    late.append((xgw, n, tp))
+                else:
+                    nc.scalar.copy(
+                        out=xgw[:, n * 512 : (n + 1) * 512].rearrange("q (g t u) -> q g t u", g=2, u=2),
+                        in_=tp[:].rearrange("q (g u) t -> q g t u", g=2),
+                    )
             xg_tiles[i] = xg
+            if i + 1 >= FIRST_PERMUTED:
+                permute_s(i + 1)
+
+        def empty_by_vector():
+            xgw, n, tp = late.pop(0)
+            nc.vector.tensor_copy(
+                out=xgw[:, n * 512 : (n + 1) * 512].rearrange("q (g t u) -> q g t u", g=2, u=2),
+                in_=tp[:].rearrange("q (g u) t -> q g t u", g=2),
+            )
 
         def new_codes(i):
             xc = work.tile([P, SUB * 256], U32, name="xc", align_bytes=64)
@@ -152,10 +183,12 @@ def tile_linear2mpo_pb_t_kernel(tc, x, t3, core4, bias, out):
                 in_=xg_tiles[i][:, n0 * 1024 : n1 * 1024],
             )
 
-        def mm(i):
+        def mm(i, n0=0, n1=SUB):
             xc, xs = xc_tiles[i]
-            acc = ps_a.tile([P, SUB, OUT], F32, name="acc", tag="acc")
-            for n in range(SUB):
+            if n0 == 0:
+                acc_tiles[i] = ps_a.tile([P, SUB, OUT], F32, name="acc", tag="acc")
+            acc = acc_tiles[i]
+            for n in range(n0, n1):
                 for g in range(2):
                     cols = slice((n * 2 + g) * 128, (n * 2 + g + 1) * 128)
                     nc.tensor.matmul_mx(
@@ -167,12 +200,13 @@ def tile_linear2mpo_pb_t_kernel(tc, x, t3, core4, bias, out):
                         start=(g == 0),
                         stop=(g == 1),
                     )
-            acc_tiles[i] = acc
 
-        def finish(i):
-            y = yout.tile([P, SUB, OUT], F32, name="y")
-            nc.vector.tensor_tensor(out=y[:], in0=acc_tiles[i][:], in1=bias_t[:], op=ADD)
-            nc.sync.dma_start(out=o_v[i], in_=y[:])
+        def finish(i, n0=0, n1=SUB):
+            if n0 == 0:
+                y_tiles[i] = yout.tile([P, SUB, OUT], F32, name="y")
+            y = y_tiles[i]
+            nc.vector.tensor_tensor(out=y[:, n0:n1], in0=acc_tiles[i][:, n0:n1], in1=bias_t[:, n0:n1], op=ADD)
+            nc.sync.dma_start(out=o_v[i][:, n0:n1], in_=y[:, n0:n1])
 
         for half in range(2):
             nc.vector.quantize_mx(

@@ -135,10 +135,12 @@ def tile_linear2mpo_pb_t_kernel(tc, x, t3, core4, bias, out):
             )
             xq_tiles[i] = xq
 
-        def transposes(i, mid_dummy, by_vector=()):
-            xg = work.tile([P, SUB * K2], BF16, name="xg", align_bytes=64)
+        def transposes(i, mid_dummy, by_vector=(), n0=0, n1=SUB):
+            if n0 == 0:
+                xg_tiles[i] = work.tile([P, SUB * K2], BF16, name="xg", align_bytes=64)
+            xg = xg_tiles[i]
             xgw = xg[:].bitcast(F32)
-            for n in range(SUB):
+            for n in range(n0, n1):
                 tp = ps_t.tile([P, 4, P], F32, name="tp", tag="tp")
                 for g in range(2):
                     for u in range(2):
@@ -159,8 +161,7 @@ def tile_linear2mpo_pb_t_kernel(tc, x, t3, core4, bias, out):
                         out=xgw[:, n * 512 : (n + 1) * 512].rearrange("q (g t u) -> q g t u", g=2, u=2),
                         in_=tp[:].rearrange("q (g u) t -> q g t u", g=2),
                     )
-            xg_tiles[i] = xg
-            if i + 1 >= FIRST_PERMUTED:
+            if n1 == SUB and i + 1 >= FIRST_PERMUTED:
                 permute_s(i + 1)
 
         def empty_by_vector():
@@ -186,8 +187,10 @@ def tile_linear2mpo_pb_t_kernel(tc, x, t3, core4, bias, out):
         def mm(i, n0=0, n1=SUB):
             xc, xs = xc_tiles[i]
             if n0 == 0:
-                acc_tiles[i] = ps_a.tile([P, SUB, OUT], F32, name="acc", tag="acc")
-            acc = acc_tiles[i]
+                acc = ps_a.tile([P, SUB, OUT], F32, name="acc", tag="acc")
+            else:
+                acc = ps_t.tile([P, SUB, OUT], F32, name="tp", tag="tp")
+            acc_tiles[(i, n0)] = acc
             for n in range(n0, n1):
                 for g in range(2):
                     cols = slice((n * 2 + g) * 128, (n * 2 + g + 1) * 128)
@@ -205,7 +208,7 @@ def tile_linear2mpo_pb_t_kernel(tc, x, t3, core4, bias, out):
             if n0 == 0:
                 y_tiles[i] = yout.tile([P, SUB, OUT], F32, name="y")
             y = y_tiles[i]
-            nc.vector.tensor_tensor(out=y[:, n0:n1], in0=acc_tiles[i][:, n0:n1], in1=bias_t[:, n0:n1], op=ADD)
+            nc.vector.tensor_tensor(out=y[:, n0:n1], in0=acc_tiles[(i, n0)][:, n0:n1], in1=bias_t[:, n0:n1], op=ADD)
             nc.sync.dma_start(out=o_v[i][:, n0:n1], in_=y[:, n0:n1])
 
         for half in range(2):
@@ -288,14 +291,16 @@ def tile_linear2mpo_pb_t_kernel(tc, x, t3, core4, bias, out):
         transposes(last, False)
         new_codes(last - 1)
         quant(last - 1, 0, 2)
+        finish(last - 2)
         quant(last - 1, 2, 4)
         new_codes(last)
         quant(last, 0, 1)
-        finish(last - 2)
         quant(last, 1, 2)
+        mm(last - 1)
+        mm(last, 0, 2)
         quant(last, 2, 3)
         quant(last, 3, 4)
-        mm(last - 1)
-        mm(last)
         finish(last - 1)
-        finish(last)
+        mm(last, 2, 4)
+        finish(last, 0, 2)
+        finish(last, 2, 4)

@@ -117,16 +117,20 @@ def tile_linear2mpo_pb_t_kernel(tc, x, t3, core4, bias, out):
         xc_tiles = {}
         acc_tiles = {}
 
+        def blocks_of_vector(i):
+            return NV + NS if i % 2 == 0 else NV
+
         def permute(i):
-            xp = work.tile([P, NV * 256], F32, name="xp")
+            nv = blocks_of_vector(i)
+            xp = work.tile([P, nv * 256], F32, name="xp")
             nc.vector.tensor_copy(
-                out=xp[:].rearrange("p (a u q) -> p u a q", a=NV, u=2),
-                in_=x_words[(i, "all")][:, V0 * 256 : (V0 + NV) * 256].rearrange("p (a q u) -> p u a q", a=NV, u=2),
+                out=xp[:].rearrange("p (a u q) -> p u a q", a=nv, u=2),
+                in_=x_words[(i, "all")][:, V0 * 256 : (V0 + nv) * 256].rearrange("p (a q u) -> p u a q", a=nv, u=2),
             )
             xp_tiles[i] = xp
 
         def permute_s(i):
-            if NS == 0 or i >= NG:
+            if NS == 0 or i >= NG or blocks_of_vector(i) > NV:
                 return
             xq = work.tile([P, NS * 256], F32, name="xq")
             nc.scalar.copy(
@@ -145,7 +149,7 @@ def tile_linear2mpo_pb_t_kernel(tc, x, t3, core4, bias, out):
                 for g in range(2):
                     for u in range(2):
                         blk = 2 * n + g
-                        if i >= FIRST_PERMUTED and V0 <= blk < V0 + NV:
+                        if i >= FIRST_PERMUTED and V0 <= blk < V0 + blocks_of_vector(i):
                             base = ((blk - V0) * 2 + u) * P
                             src = xp_tiles[i][:, base : base + P]
                         elif i >= FIRST_PERMUTED and S0 <= blk < S0 + NS:

@@ -15,13 +15,16 @@ TOKENS = 8192
 K2 = 1024
 OUT = 128
 SUB = 4
-GROUP = P * SUB
-NG = TOKENS // GROUP
-BANK_DT = BF16
+NG = TOKENS // (P * SUB)
+PASSES = K2 // 512
+WORDS = K2 // 2
+CODES = PASSES * P
+
+BLOCK = 256
 PIECES = {0: 4, 1: 2, 2: 2}
-FIRST_PERMUTED = 3
-V0, NV = 4, 3
-S0, NS = 7, 1
+FIRST_REORDERED = 3
+FIRST_BLOCK = 4
+SCALAR_BLOCK = 7
 
 FLOPS = 2 * 1024 * 512 * 128 + 2 * TOKENS * K2 * OUT
 
@@ -44,10 +47,9 @@ def tile_linear2mpo_pb_t_kernel(tc, x, t3, core4, bias, out):
         ctx.enter_context(tc.manual_schedule())
 
         brow = keep.tile([P, OUT], BF16, name="brow")
-        wide = keep.tile([P, 512], BF16, name="wide")
-        nc.vector.memset(wide[:], 1.0)
+        ones = keep.tile([P, 128], BF16, name="ones")
+        nc.vector.memset(ones[:], 1.0)
         nc.vector.memset(brow[:], 0.0)
-        ones = wide[:, 0:P]
         ident = keep.tile([P, P], F32, name="ident")
         make_identity(nc, ident[:])
 
@@ -59,7 +61,8 @@ def tile_linear2mpo_pb_t_kernel(tc, x, t3, core4, bias, out):
         for b in range(4):
             nc.sync.dma_start(out=t3_sb[:, b], in_=t3_v[b])
 
-        x_words = {}
+        sub_words = {}
+        group_words = {}
 
         def load_x(i):
             pieces = PIECES.get(i, 1)
@@ -67,11 +70,11 @@ def tile_linear2mpo_pb_t_kernel(tc, x, t3, core4, bias, out):
             for c in range(pieces):
                 x_sb = xin.tile([P, per, K2], BF16, name="x_sb")
                 nc.sync.dma_start(out=x_sb[:], in_=x_v[i][:, c * per : (c + 1) * per, :])
-                xw = x_sb[:].rearrange("p n k -> p (n k)").bitcast(F32)
+                words = x_sb[:].rearrange("p n k -> p (n k)").bitcast(F32)
                 for n in range(per):
-                    x_words[(i, c * per + n)] = xw[:, n * 512 : (n + 1) * 512]
+                    sub_words[(i, c * per + n)] = words[:, n * WORDS : (n + 1) * WORDS]
                 if pieces == 1:
-                    x_words[(i, "all")] = xw
+                    group_words[i] = words
 
         for i in range(7):
             load_x(i)
@@ -94,125 +97,115 @@ def tile_linear2mpo_pb_t_kernel(tc, x, t3, core4, bias, out):
             tp = ps_t.tile([P, 4, P], F32, name="tp", tag="tp")
             for h in range(2):
                 for u in range(2):
-                    base = (b * 2 + h) * 256
-                    nc.tensor.transpose(tp[:, 2 * h + u, :], t3w[:, base + u : base + 256 : 2], ident[:])
-            src = tp[:].rearrange("q s (j o) -> q j o s", j=8)
+                    base = (b * 2 + h) * BLOCK
+                    nc.tensor.transpose(tp[:, 2 * h + u, :], t3w[:, base + u : base + BLOCK : 2], ident[:])
+            turned = tp[:].rearrange("q s (j o) -> q j o s", j=8)
             if b % 2 == 0:
-                nc.scalar.copy(out=t3gw[:, :, b], in_=src)
+                nc.scalar.copy(out=t3gw[:, :, b], in_=turned)
             else:
-                nc.vector.tensor_copy(out=t3gw[:, :, b], in_=src)
+                nc.vector.tensor_copy(out=t3gw[:, :, b], in_=turned)
             if b == 1:
                 pb = ps_a.tile([P, OUT], F32, name="pb", tag="acc")
-                nc.tensor.matmul(pb[:], lhsT=ones, rhs=brow[:], start=True, stop=True)
+                nc.tensor.matmul(pb[:], lhsT=ones[:, 0:P], rhs=brow[:], start=True, stop=True)
                 for n in range(SUB):
                     nc.scalar.copy(out=bias_t[:, n, :], in_=pb[:])
         t3c = keep.tile([P, 1024], U32, name="t3c", align_bytes=64)
         t3s = keep.tile([P, 1024], U8, name="t3s", align_bytes=64)
 
-        xp_tiles = {}
-        late = []
-        y_tiles = {}
-        xq_tiles = {}
-        xg_tiles = {}
-        xc_tiles = {}
-        acc_tiles = {}
+        by_vector = {}
+        by_scalar = {}
+        turned_x = {}
+        codes = {}
+        sums = {}
+        results = {}
 
-        def blocks_of_vector(i):
-            return NV + NS if i % 2 == 0 else NV
+        def vector_blocks(i):
+            return SCALAR_BLOCK - FIRST_BLOCK + (1 if i % 2 == 0 else 0)
 
-        def permute(i):
-            nv = blocks_of_vector(i)
-            xp = work.tile([P, nv * 256], F32, name="xp")
+        def reorder(i):
+            nb = vector_blocks(i)
+            xp = work.tile([P, nb * BLOCK], F32, name="xp")
             nc.vector.tensor_copy(
-                out=xp[:].rearrange("p (a u q) -> p u a q", a=nv, u=2),
-                in_=x_words[(i, "all")][:, V0 * 256 : (V0 + nv) * 256].rearrange("p (a q u) -> p u a q", a=nv, u=2),
+                out=xp[:].rearrange("p (a u q) -> p u a q", a=nb, u=2),
+                in_=group_words[i][:, FIRST_BLOCK * BLOCK : (FIRST_BLOCK + nb) * BLOCK].rearrange(
+                    "p (a q u) -> p u a q", a=nb, u=2
+                ),
             )
-            xp_tiles[i] = xp
+            by_vector[i] = xp
 
-        def permute_s(i):
-            if NS == 0 or i >= NG or blocks_of_vector(i) > NV:
-                return
-            xq = work.tile([P, NS * 256], F32, name="xq")
+        def reorder_by_scalar(i):
+            xq = work.tile([P, BLOCK], F32, name="xq")
             nc.scalar.copy(
-                out=xq[:].rearrange("p (a u q) -> p a u q", a=NS, u=2),
-                in_=x_words[(i, "all")][:, S0 * 256 : (S0 + NS) * 256].rearrange("p (a q u) -> p a u q", a=NS, u=2),
+                out=xq[:].rearrange("p (a u q) -> p a u q", a=1, u=2),
+                in_=group_words[i][:, SCALAR_BLOCK * BLOCK : (SCALAR_BLOCK + 1) * BLOCK].rearrange(
+                    "p (a q u) -> p a u q", a=1, u=2
+                ),
             )
-            xq_tiles[i] = xq
+            by_scalar[i] = xq
 
-        def transposes(i, mid_dummy, by_vector=(), n0=0, n1=SUB):
-            if n0 == 0:
-                xg_tiles[i] = work.tile([P, SUB * K2], BF16, name="xg", align_bytes=64)
-            xg = xg_tiles[i]
+        def transposes(i):
+            xg = work.tile([P, SUB * K2], BF16, name="xg", align_bytes=64)
             xgw = xg[:].bitcast(F32)
-            for n in range(n0, n1):
+            for n in range(SUB):
                 tp = ps_t.tile([P, 4, P], F32, name="tp", tag="tp")
                 for g in range(2):
                     for u in range(2):
                         blk = 2 * n + g
-                        if i >= FIRST_PERMUTED and V0 <= blk < V0 + blocks_of_vector(i):
-                            base = ((blk - V0) * 2 + u) * P
-                            src = xp_tiles[i][:, base : base + P]
-                        elif i >= FIRST_PERMUTED and S0 <= blk < S0 + NS:
-                            base = ((blk - S0) * 2 + u) * P
-                            src = xq_tiles[i][:, base : base + P]
+                        if i >= FIRST_REORDERED and FIRST_BLOCK <= blk < FIRST_BLOCK + vector_blocks(i):
+                            base = ((blk - FIRST_BLOCK) * 2 + u) * P
+                            src = by_vector[i][:, base : base + P]
+                        elif i >= FIRST_REORDERED and blk == SCALAR_BLOCK:
+                            src = by_scalar[i][:, u * P : (u + 1) * P]
                         else:
-                            src = x_words[(i, n)][:, g * 256 + u : (g + 1) * 256 : 2]
+                            src = sub_words[(i, n)][:, g * BLOCK + u : (g + 1) * BLOCK : 2]
                         nc.tensor.transpose(tp[:, 2 * g + u, :], src, ident[:])
-                if n in by_vector:
-                    late.append((xgw, n, tp))
-                else:
-                    nc.scalar.copy(
-                        out=xgw[:, n * 512 : (n + 1) * 512].rearrange("q (g t u) -> q g t u", g=2, u=2),
-                        in_=tp[:].rearrange("q (g u) t -> q g t u", g=2),
-                    )
-            if n1 == SUB and i + 1 >= FIRST_PERMUTED:
-                permute_s(i + 1)
-
-        def empty_by_vector():
-            xgw, n, tp = late.pop(0)
-            nc.vector.tensor_copy(
-                out=xgw[:, n * 512 : (n + 1) * 512].rearrange("q (g t u) -> q g t u", g=2, u=2),
-                in_=tp[:].rearrange("q (g u) t -> q g t u", g=2),
-            )
+                nc.scalar.copy(
+                    out=xgw[:, n * WORDS : (n + 1) * WORDS].rearrange("q (g t u) -> q g t u", g=2, u=2),
+                    in_=tp[:].rearrange("q (g u) t -> q g t u", g=2),
+                )
+            turned_x[i] = xg
+            if FIRST_REORDERED <= i + 1 < NG and (i + 1) % 2 == 1:
+                reorder_by_scalar(i + 1)
 
         def new_codes(i):
-            xc = work.tile([P, SUB * 256], U32, name="xc", align_bytes=64)
-            xs = work.tile([P, SUB * 256], U8, name="xs", align_bytes=64)
-            xc_tiles[i] = (xc, xs)
+            xc = work.tile([P, SUB * CODES], U32, name="xc", align_bytes=64)
+            xs = work.tile([P, SUB * CODES], U8, name="xs", align_bytes=64)
+            codes[i] = (xc, xs)
 
-        def quant(i, n0, n1):
-            xc, xs = xc_tiles[i]
+        def quantise(i, n0, n1):
+            xc, xs = codes[i]
             nc.vector.quantize_mx(
-                out=xc[:, n0 * 256 : n1 * 256].bitcast(FP8X4),
-                scales=xs[:, n0 * 256 : n1 * 256],
-                in_=xg_tiles[i][:, n0 * 1024 : n1 * 1024],
+                out=xc[:, n0 * CODES : n1 * CODES].bitcast(FP8X4),
+                scales=xs[:, n0 * CODES : n1 * CODES],
+                in_=turned_x[i][:, n0 * 4 * CODES : n1 * 4 * CODES],
             )
 
-        def mm(i, n0=0, n1=SUB):
-            xc, xs = xc_tiles[i]
+        def multiply(i, n0=0, n1=SUB):
+            xc, xs = codes[i]
             if n0 == 0:
                 acc = ps_a.tile([P, SUB, OUT], F32, name="acc", tag="acc")
             else:
                 acc = ps_t.tile([P, SUB, OUT], F32, name="tp", tag="tp")
-            acc_tiles[(i, n0)] = acc
+            sums[(i, n0)] = acc
             for n in range(n0, n1):
-                for g in range(2):
-                    cols = slice((n * 2 + g) * 128, (n * 2 + g + 1) * 128)
+                for g in range(PASSES):
+                    tokens = slice((n * PASSES + g) * P, (n * PASSES + g + 1) * P)
+                    channels = slice(g * OUT, (g + 1) * OUT)
                     nc.tensor.matmul_mx(
                         out=acc[:, n, :],
-                        lhsT=xc[:, cols].bitcast(FP8X4),
-                        lhsT_scale=xs[:, cols],
-                        rhs=mc[:, g * 128 : (g + 1) * 128].bitcast(FP8X4),
-                        rhs_scale=ms[:, g * 128 : (g + 1) * 128],
+                        lhsT=xc[:, tokens].bitcast(FP8X4),
+                        lhsT_scale=xs[:, tokens],
+                        rhs=mc[:, channels].bitcast(FP8X4),
+                        rhs_scale=ms[:, channels],
                         start=(g == 0),
-                        stop=(g == 1),
+                        stop=(g == PASSES - 1),
                     )
 
         def finish(i, n0=0, n1=SUB):
             if n0 == 0:
-                y_tiles[i] = yout.tile([P, SUB, OUT], F32, name="y")
-            y = y_tiles[i]
-            nc.vector.tensor_tensor(out=y[:, n0:n1], in0=acc_tiles[(i, n0)][:, n0:n1], in1=bias_t[:, n0:n1], op=ADD)
+                results[i] = yout.tile([P, SUB, OUT], F32, name="y")
+            y = results[i]
+            nc.vector.tensor_tensor(out=y[:, n0:n1], in0=sums[(i, n0)][:, n0:n1], in1=bias_t[:, n0:n1], op=ADD)
             nc.sync.dma_start(out=o_v[i][:, n0:n1], in_=y[:, n0:n1])
 
         for half in range(2):
@@ -221,7 +214,7 @@ def tile_linear2mpo_pb_t_kernel(tc, x, t3, core4, bias, out):
                 scales=t3s[:, half * 512 : (half + 1) * 512],
                 in_=t3g[:, half * 2048 : (half + 1) * 2048],
             )
-        transposes(0, True)
+        transposes(0)
         for i in range(7, 11):
             load_x(i)
 
@@ -229,7 +222,7 @@ def tile_linear2mpo_pb_t_kernel(tc, x, t3, core4, bias, out):
         mAv = mA[:].rearrange("m (x j i) -> m x j i", x=32, j=8, i=4)
         pms = []
         for hh in range(2):
-            pm = ps_a.tile([P, 4, 128], BANK_DT, name="pm", tag="acc")
+            pm = ps_a.tile([P, 4, 128], BF16, name="pm", tag="acc")
             for jj in range(4):
                 j = hh * 4 + jj
                 nc.tensor.matmul_mx(
@@ -244,17 +237,17 @@ def tile_linear2mpo_pb_t_kernel(tc, x, t3, core4, bias, out):
             pms.append(pm)
         new_codes(0)
         for n in range(SUB):
-            quant(0, n, n + 1)
+            quantise(0, n, n + 1)
         nc.scalar.copy(out=mAv[:, :, 0:4, :], in_=pms[0][:].rearrange("m j (x i) -> m x j i", i=4))
         nc.vector.tensor_copy(out=mAv[:, :, 4:8, :], in_=pms[1][:].rearrange("m j (x i) -> m x j i", i=4))
 
-        transposes(1, True)
+        transposes(1)
         for i in range(11, 13):
             load_x(i)
         mB = keep.tile([P, 1024], BF16, name="mB", align_bytes=64)
         mG = keep.tile([P, 1024], BF16, name="mG", align_bytes=64)
-        mc = keep.tile([P, 256], U32, name="mc", align_bytes=64)
-        ms = keep.tile([P, 256], U8, name="ms", align_bytes=64)
+        mc = keep.tile([P, PASSES * OUT], U32, name="mc", align_bytes=64)
+        ms = keep.tile([P, PASSES * OUT], U8, name="ms", align_bytes=64)
         nc.vector.transpose(out=mB[:], in_=mA[:])
         mGv = mG[:].rearrange("p (g a o t) -> p g a o t", g=2, a=16, o=8, t=4)
         mBv = mB[:].rearrange("p (t o a g) -> p g a o t", t=4, o=8, a=16, g=2)
@@ -262,49 +255,49 @@ def tile_linear2mpo_pb_t_kernel(tc, x, t3, core4, bias, out):
             nc.vector.tensor_copy(out=mGv[:, g], in_=mBv[:, g])
         nc.vector.quantize_mx(out=mc[:].bitcast(FP8X4), scales=ms[:], in_=mG[:])
 
-        transposes(2, False)
+        transposes(2)
         for i in range(13, 15):
             load_x(i)
-        mm(0)
+        multiply(0)
         new_codes(1)
-        quant(1, 0, 2)
-        quant(1, 2, 4)
-        permute(3)
+        quantise(1, 0, 2)
+        quantise(1, 2, 4)
+        reorder(3)
 
-        transposes(3, False)
+        transposes(3)
         load_x(15)
         new_codes(2)
-        quant(2, 0, 2)
-        quant(2, 2, 4)
-        mm(1)
+        quantise(2, 0, 2)
+        quantise(2, 2, 4)
+        multiply(1)
         finish(0)
-        mm(2)
+        multiply(2)
         finish(1)
-        permute(4)
+        reorder(4)
 
-        for tick in range(4, NG - 1):
-            transposes(tick, False)
-            new_codes(tick - 1)
-            quant(tick - 1, 0, 2)
-            quant(tick - 1, 2, 4)
-            mm(tick - 1)
-            finish(tick - 2)
-            permute(tick + 1)
+        for i in range(4, NG - 1):
+            transposes(i)
+            new_codes(i - 1)
+            quantise(i - 1, 0, 2)
+            quantise(i - 1, 2, 4)
+            multiply(i - 1)
+            finish(i - 2)
+            reorder(i + 1)
 
         last = NG - 1
-        transposes(last, False)
+        transposes(last)
         new_codes(last - 1)
-        quant(last - 1, 0, 2)
+        quantise(last - 1, 0, 2)
         finish(last - 2)
-        quant(last - 1, 2, 4)
+        quantise(last - 1, 2, 4)
         new_codes(last)
-        quant(last, 0, 1)
-        quant(last, 1, 2)
-        mm(last - 1)
-        mm(last, 0, 2)
-        quant(last, 2, 3)
-        quant(last, 3, 4)
+        quantise(last, 0, 1)
+        quantise(last, 1, 2)
+        multiply(last - 1)
+        multiply(last, 0, 2)
+        quantise(last, 2, 3)
+        quantise(last, 3, 4)
         finish(last - 1)
-        mm(last, 2, 4)
+        multiply(last, 2, 4)
         finish(last, 0, 2)
         finish(last, 2, 4)

@@ -120,7 +120,7 @@ def tile_linear2mpo_pb_t_kernel(tc, x, t3, core4, bias, out):
         results = {}
 
         def vector_blocks(i):
-            return SCALAR_BLOCK - FIRST_BLOCK + (1 if i % 2 == 0 else 0)
+            return SCALAR_BLOCK - FIRST_BLOCK
 
         def reorder(i):
             nb = vector_blocks(i)
@@ -154,7 +154,7 @@ def tile_linear2mpo_pb_t_kernel(tc, x, t3, core4, bias, out):
                         if i >= FIRST_REORDERED and FIRST_BLOCK <= blk < FIRST_BLOCK + vector_blocks(i):
                             base = ((blk - FIRST_BLOCK) * 2 + u) * P
                             src = by_vector[i][:, base : base + P]
-                        elif i >= FIRST_REORDERED and blk == SCALAR_BLOCK:
+                        elif i >= FIRST_REORDERED and blk == SCALAR_BLOCK and i % 2 == 1:
                             src = by_scalar[i][:, u * P : (u + 1) * P]
                         else:
                             src = sub_words[(i, n)][:, g * BLOCK + u : (g + 1) * BLOCK : 2]

@@ -33,7 +33,7 @@ def tile_linear2mpo_pb_t_kernel(tc, x, t3, core4, bias, out):
     nc = tc.nc
     x_v = x.flatten_outer_dims().rearrange("(g p n) k -> g p n k", p=P, n=SUB)
     o_v = out.flatten_outer_dims().rearrange("(g p n) c -> g p n c", p=P, n=SUB)
-    t3_v = t3.rearrange("(h b c) o r -> b (c o) h r", h=2, b=4)
+    t3_v = t3.rearrange("(a i) (o e) r -> a (i o) e r", a=4, e=2)
     c4_v = core4.rearrange("(p j) i o z -> p j (i o z)", j=4)
     bias_v = bias.rearrange("(a n) -> a n", a=1)
 
@@ -79,7 +79,7 @@ def tile_linear2mpo_pb_t_kernel(tc, x, t3, core4, bias, out):
         for i in range(7):
             load_x(i)
 
-        bias_t = keep.tile([P, SUB, OUT], F32, name="bias_t")
+        bias_t = keep.tile([P, OUT], F32, name="bias_t")
 
         c4g = keep.tile([P, 512], BF16, name="c4g", align_bytes=64)
         nc.scalar.copy(
@@ -92,23 +92,22 @@ def tile_linear2mpo_pb_t_kernel(tc, x, t3, core4, bias, out):
 
         t3w = t3_sb[:].rearrange("p b h r -> p (b h r)").bitcast(F32)
         t3g = keep.tile([P, 4096], BF16, name="t3g", align_bytes=64)
-        t3gw = t3g[:].bitcast(F32).rearrange("q (j b o s) -> q j b o s", j=8, b=4, o=16, s=4)
+        t3gw = t3g[:].bitcast(F32).rearrange("q (j c d h o s) -> q j c d h o s", j=8, c=2, d=2, h=2, o=8, s=4)
         for b in range(4):
             tp = ps_t.tile([P, 4, P], F32, name="tp", tag="tp")
             for h in range(2):
                 for u in range(2):
                     base = (b * 2 + h) * BLOCK
                     nc.tensor.transpose(tp[:, 2 * h + u, :], t3w[:, base + u : base + BLOCK : 2], ident[:])
-            turned = tp[:].rearrange("q s (j o) -> q j o s", j=8)
+            turned = tp[:].rearrange("q s (d j o) -> q j d o s", d=2, j=8)
             if b % 2 == 0:
-                nc.scalar.copy(out=t3gw[:, :, b], in_=turned)
+                nc.scalar.copy(out=t3gw[:, :, b % 2, :, b // 2], in_=turned)
             else:
-                nc.vector.tensor_copy(out=t3gw[:, :, b], in_=turned)
+                nc.vector.tensor_copy(out=t3gw[:, :, b % 2, :, b // 2], in_=turned)
             if b == 1:
                 pb = ps_a.tile([P, OUT], F32, name="pb", tag="acc")
                 nc.tensor.matmul(pb[:], lhsT=ones[:, 0:P], rhs=brow[:], start=True, stop=True)
-                for n in range(SUB):
-                    nc.scalar.copy(out=bias_t[:, n, :], in_=pb[:])
+                nc.scalar.copy(out=bias_t[:], in_=pb[:])
         t3c = keep.tile([P, 1024], U32, name="t3c", align_bytes=64)
         t3s = keep.tile([P, 1024], U8, name="t3s", align_bytes=64)
 
@@ -205,7 +204,8 @@ def tile_linear2mpo_pb_t_kernel(tc, x, t3, core4, bias, out):
             if n0 == 0:
                 results[i] = yout.tile([P, SUB, OUT], F32, name="y")
             y = results[i]
-            nc.vector.tensor_tensor(out=y[:, n0:n1], in0=sums[(i, n0)][:, n0:n1], in1=bias_t[:, n0:n1], op=ADD)
+            spread = bias_t[:].unsqueeze(1).to_broadcast([P, n1 - n0, OUT])
+            nc.vector.tensor_tensor(out=y[:, n0:n1], in0=sums[(i, n0)][:, n0:n1], in1=spread, op=ADD)
             nc.sync.dma_start(out=o_v[i][:, n0:n1], in_=y[:, n0:n1])
 
         for half in range(2):
@@ -250,7 +250,7 @@ def tile_linear2mpo_pb_t_kernel(tc, x, t3, core4, bias, out):
         ms = keep.tile([P, PASSES * OUT], U8, name="ms", align_bytes=64)
         nc.vector.transpose(out=mB[:], in_=mA[:])
         mGv = mG[:].rearrange("p (g a o t) -> p g a o t", g=2, a=16, o=8, t=4)
-        mBv = mB[:].rearrange("p (t o a g) -> p g a o t", t=4, o=8, a=16, g=2)
+        mBv = mB[:].rearrange("p (t o g a) -> p g a o t", t=4, o=8, a=16, g=2)
         for g in range(2):
             nc.vector.tensor_copy(out=mGv[:, g], in_=mBv[:, g])
         nc.vector.quantize_mx(out=mc[:].bitcast(FP8X4), scales=ms[:], in_=mG[:])

@@ -61,20 +61,26 @@ def tile_linear2mpo_pb_t_kernel(tc, x, t3, core4, bias, out):
         for b in range(4):
             nc.sync.dma_start(out=t3_sb[:, b], in_=t3_v[b])
 
-        sub_words = {}
+        block_words = {}
         group_words = {}
 
         def load_x(i):
             pieces = PIECES.get(i, 1)
             per = SUB // pieces
             for c in range(pieces):
-                x_sb = xin.tile([P, per, K2], BF16, name="x_sb")
-                nc.sync.dma_start(out=x_sb[:], in_=x_v[i][:, c * per : (c + 1) * per, :])
-                words = x_sb[:].rearrange("p n k -> p (n k)").bitcast(F32)
-                for n in range(per):
-                    sub_words[(i, c * per + n)] = words[:, n * WORDS : (n + 1) * WORDS]
-                if pieces == 1:
-                    group_words[i] = words
+                if i == 0 and c == pieces - 1:
+                    for g in range(PASSES):
+                        x_half = xin.tile([P, 1, 512], BF16, name="x_sb")
+                        nc.sync.dma_start(out=x_half[:], in_=x_v[i][:, c : c + 1, g * 512 : (g + 1) * 512])
+                        block_words[(i, 2 * c + g)] = x_half[:].rearrange("p n k -> p (n k)").bitcast(F32)
+                else:
+                    x_sb = xin.tile([P, per, K2], BF16, name="x_sb")
+                    nc.sync.dma_start(out=x_sb[:], in_=x_v[i][:, c * per : (c + 1) * per, :])
+                    words = x_sb[:].rearrange("p n k -> p (n k)").bitcast(F32)
+                    for blk in range(2 * per):
+                        block_words[(i, 2 * c * per + blk)] = words[:, blk * BLOCK : (blk + 1) * BLOCK]
+                    if pieces == 1:
+                        group_words[i] = words
 
         for i in range(7):
             load_x(i)
@@ -156,7 +162,7 @@ def tile_linear2mpo_pb_t_kernel(tc, x, t3, core4, bias, out):
                         elif i >= FIRST_REORDERED and blk == SCALAR_BLOCK and i % 2 == 1:
                             src = by_scalar[i][:, u * P : (u + 1) * P]
                         else:
-                            src = sub_words[(i, n)][:, g * BLOCK + u : (g + 1) * BLOCK : 2]
+                            src = block_words[(i, blk)][:, u:BLOCK:2]
                         nc.tensor.transpose(tp[:, 2 * g + u, :], src, ident[:])
                 nc.scalar.copy(
                     out=xgw[:, n * WORDS : (n + 1) * WORDS].rearrange("q (g t u) -> q g t u", g=2, u=2),

from contextlib import ExitStack

import concourse.mybir as mybir
from concourse.masks import make_identity

F32 = mybir.dt.float32
BF16 = mybir.dt.bfloat16
U32 = mybir.dt.uint32
U8 = mybir.dt.uint8
FP8X4 = mybir.dt.float8_e4m3fn_x4
ADD = mybir.AluOpType.add

P = 128
TOKENS = 8192
K2 = 1024
OUT = 128
SUB = 4
NG = TOKENS // (P * SUB)
PASSES = K2 // 512
WORDS = K2 // 2
CODES = PASSES * P

BLOCK = 256
PIECES = {0: 4, 1: 2, 2: 2}
FIRST_REORDERED = 3
FIRST_BLOCK = 4
SCALAR_BLOCK = 7

FLOPS = 2 * 1024 * 512 * 128 + 2 * TOKENS * K2 * OUT


def tile_linear2mpo_pb_t_kernel(tc, x, t3, core4, bias, out):
    nc = tc.nc
    x_v = x.flatten_outer_dims().rearrange("(g p n) k -> g p n k", p=P, n=SUB)
    o_v = out.flatten_outer_dims().rearrange("(g p n) c -> g p n c", p=P, n=SUB)
    t3_v = t3.rearrange("(a i) (o e) r -> a (i o) e r", a=4, e=2)
    c4_v = core4.rearrange("(p j) i o z -> p j (i o z)", j=4)
    bias_v = bias.rearrange("(a n) -> a n", a=1)

    with ExitStack() as ctx:
        keep = ctx.enter_context(tc.tile_pool(name="keep", bufs=1))
        xin = ctx.enter_context(tc.tile_pool(name="xin", bufs=12))
        work = ctx.enter_context(tc.tile_pool(name="work", bufs=3))
        yout = ctx.enter_context(tc.tile_pool(name="yout", bufs=NG))
        ps_t = ctx.enter_context(tc.psum_pool(name="ps_t", bufs=6))
        ps_a = ctx.enter_context(tc.psum_pool(name="ps_a", bufs=2))
        ctx.enter_context(tc.manual_schedule())

        brow = keep.tile([P, OUT], BF16, name="brow")
        ones = keep.tile([P, 128], BF16, name="ones")
        nc.vector.memset(ones[:], 1.0)
        nc.vector.memset(brow[:], 0.0)
        ident = keep.tile([P, P], F32, name="ident")
        make_identity(nc, ident[:])

        c4_sb = keep.tile([P, 4, 128], BF16, name="c4_sb")
        nc.scalar.dma_start(out=c4_sb[:], in_=c4_v)
        nc.scalar.dma_start(out=brow[0:1, :], in_=bias_v)

        t3_sb = keep.tile([P, 4, 2, 512], BF16, name="t3_sb")
        for b in range(4):
            nc.sync.dma_start(out=t3_sb[:, b], in_=t3_v[b])

        block_words = {}
        group_words = {}

        def load_x(i):
            pieces = PIECES.get(i, 1)
            per = SUB // pieces
            for c in range(pieces):
                if i == 0 and c == pieces - 1:
                    for g in range(PASSES):
                        x_half = xin.tile([P, 1, 512], BF16, name="x_sb")
                        nc.sync.dma_start(out=x_half[:], in_=x_v[i][:, c : c + 1, g * 512 : (g + 1) * 512])
                        block_words[(i, 2 * c + g)] = x_half[:].rearrange("p n k -> p (n k)").bitcast(F32)
                else:
                    x_sb = xin.tile([P, per, K2], BF16, name="x_sb")
                    nc.sync.dma_start(out=x_sb[:], in_=x_v[i][:, c * per : (c + 1) * per, :])
                    words = x_sb[:].rearrange("p n k -> p (n k)").bitcast(F32)
                    for blk in range(2 * per):
                        block_words[(i, 2 * c * per + blk)] = words[:, blk * BLOCK : (blk + 1) * BLOCK]
                    if pieces == 1:
                        group_words[i] = words

        for i in range(7):
            load_x(i)

        bias_t = keep.tile([P, OUT], F32, name="bias_t")

        c4g = keep.tile([P, 512], BF16, name="c4g", align_bytes=64)
        nc.scalar.copy(
            out=c4g[:].rearrange("p (x h j) -> p x h j", x=32, h=4, j=4),
            in_=c4_sb[:].rearrange("p j (h x) -> p x h j", h=4),
        )
        c4c = keep.tile([P, 128], U32, name="c4c", align_bytes=64)
        c4s = keep.tile([P, 128], U8, name="c4s", align_bytes=64)
        nc.vector.quantize_mx(out=c4c[:].bitcast(FP8X4), scales=c4s[:], in_=c4g[:])

        t3w = t3_sb[:].rearrange("p b h r -> p (b h r)").bitcast(F32)
        t3g = keep.tile([P, 4096], BF16, name="t3g", align_bytes=64)
        t3gw = t3g[:].bitcast(F32).rearrange("q (j c d h o s) -> q j c d h o s", j=8, c=2, d=2, h=2, o=8, s=4)
        for b in range(4):
            tp = ps_t.tile([P, 4, P], F32, name="tp", tag="tp")
            for h in range(2):
                for u in range(2):
                    base = (b * 2 + h) * BLOCK
                    nc.tensor.transpose(tp[:, 2 * h + u, :], t3w[:, base + u : base + BLOCK : 2], ident[:])
            turned = tp[:].rearrange("q s (d j o) -> q j d o s", d=2, j=8)
            if b % 2 == 0:
                nc.scalar.copy(out=t3gw[:, :, b % 2, :, b // 2], in_=turned)
            else:
                nc.vector.tensor_copy(out=t3gw[:, :, b % 2, :, b // 2], in_=turned)
            if b == 1:
                pb = ps_a.tile([P, OUT], F32, name="pb", tag="acc")
                nc.tensor.matmul(pb[:], lhsT=ones[:, 0:P], rhs=brow[:], start=True, stop=True)
                nc.scalar.copy(out=bias_t[:], in_=pb[:])
        t3c = keep.tile([P, 1024], U32, name="t3c", align_bytes=64)
        t3s = keep.tile([P, 1024], U8, name="t3s", align_bytes=64)

        by_vector = {}
        by_scalar = {}
        turned_x = {}
        codes = {}
        sums = {}
        results = {}

        def vector_blocks(i):
            return SCALAR_BLOCK - FIRST_BLOCK

        def reorder(i):
            nb = vector_blocks(i)
            xp = work.tile([P, nb * BLOCK], F32, name="xp")
            nc.vector.tensor_copy(
                out=xp[:].rearrange("p (a u q) -> p u a q", a=nb, u=2),
                in_=group_words[i][:, FIRST_BLOCK * BLOCK : (FIRST_BLOCK + nb) * BLOCK].rearrange(
                    "p (a q u) -> p u a q", a=nb, u=2
                ),
            )
            by_vector[i] = xp

        def reorder_by_scalar(i):
            xq = work.tile([P, BLOCK], F32, name="xq")
            nc.scalar.copy(
                out=xq[:].rearrange("p (a u q) -> p a u q", a=1, u=2),
                in_=group_words[i][:, SCALAR_BLOCK * BLOCK : (SCALAR_BLOCK + 1) * BLOCK].rearrange(
                    "p (a q u) -> p a u q", a=1, u=2
                ),
            )
            by_scalar[i] = xq

        def transposes(i):
            xg = work.tile([P, SUB * K2], BF16, name="xg", align_bytes=64)
            xgw = xg[:].bitcast(F32)
            for n in range(SUB):
                tp = ps_t.tile([P, 4, P], F32, name="tp", tag="tp")
                for g in range(2):
                    for u in range(2):
                        blk = 2 * n + g
                        if i >= FIRST_REORDERED and FIRST_BLOCK <= blk < FIRST_BLOCK + vector_blocks(i):
                            base = ((blk - FIRST_BLOCK) * 2 + u) * P
                            src = by_vector[i][:, base : base + P]
                        elif i >= FIRST_REORDERED and blk == SCALAR_BLOCK and i % 2 == 1:
                            src = by_scalar[i][:, u * P : (u + 1) * P]
                        else:
                            src = block_words[(i, blk)][:, u:BLOCK:2]
                        nc.tensor.transpose(tp[:, 2 * g + u, :], src, ident[:])
                nc.scalar.copy(
                    out=xgw[:, n * WORDS : (n + 1) * WORDS].rearrange("q (g t u) -> q g t u", g=2, u=2),
                    in_=tp[:].rearrange("q (g u) t -> q g t u", g=2),
                )
            turned_x[i] = xg
            if FIRST_REORDERED <= i + 1 < NG and (i + 1) % 2 == 1:
                reorder_by_scalar(i + 1)

        def new_codes(i):
            xc = work.tile([P, SUB * CODES], U32, name="xc", align_bytes=64)
            xs = work.tile([P, SUB * CODES], U8, name="xs", align_bytes=64)
            codes[i] = (xc, xs)

        def quantise(i, n0, n1):
            xc, xs = codes[i]
            nc.vector.quantize_mx(
                out=xc[:, n0 * CODES : n1 * CODES].bitcast(FP8X4),
                scales=xs[:, n0 * CODES : n1 * CODES],
                in_=turned_x[i][:, n0 * 4 * CODES : n1 * 4 * CODES],
            )

        def multiply(i, n0=0, n1=SUB):
            xc, xs = codes[i]
            if n0 == 0:
                acc = ps_a.tile([P, SUB, OUT], F32, name="acc", tag="acc")
            else:
                acc = ps_t.tile([P, SUB, OUT], F32, name="tp", tag="tp")
            sums[(i, n0)] = acc
            for n in range(n0, n1):
                for g in range(PASSES):
                    tokens = slice((n * PASSES + g) * P, (n * PASSES + g + 1) * P)
                    channels = slice(g * OUT, (g + 1) * OUT)
                    nc.tensor.matmul_mx(
                        out=acc[:, n, :],
                        lhsT=xc[:, tokens].bitcast(FP8X4),
                        lhsT_scale=xs[:, tokens],
                        rhs=mc[:, channels].bitcast(FP8X4),
                        rhs_scale=ms[:, channels],
                        start=(g == 0),
                        stop=(g == PASSES - 1),
                    )

        def finish(i, n0=0, n1=SUB):
            if n0 == 0:
                results[i] = yout.tile([P, SUB, OUT], F32, name="y")
            y = results[i]
            spread = bias_t[:].unsqueeze(1).to_broadcast([P, n1 - n0, OUT])
            nc.vector.tensor_tensor(out=y[:, n0:n1], in0=sums[(i, n0)][:, n0:n1], in1=spread, op=ADD)
            nc.sync.dma_start(out=o_v[i][:, n0:n1], in_=y[:, n0:n1])

        for half in range(2):
            nc.vector.quantize_mx(
                out=t3c[:, half * 512 : (half + 1) * 512].bitcast(FP8X4),
                scales=t3s[:, half * 512 : (half + 1) * 512],
                in_=t3g[:, half * 2048 : (half + 1) * 2048],
            )
        transposes(0)
        for i in range(7, 11):
            load_x(i)

        mA = keep.tile([P, 1024], BF16, name="mA", align_bytes=64)
        mAv = mA[:].rearrange("m (x j i) -> m x j i", x=32, j=8, i=4)
        pms = []
        for hh in range(2):
            pm = ps_a.tile([P, 4, 128], BF16, name="pm", tag="acc")
            for jj in range(4):
                j = hh * 4 + jj
                nc.tensor.matmul_mx(
                    out=pm[:, jj, :],
                    lhsT=t3c[:, j * 128 : (j + 1) * 128].bitcast(FP8X4),
                    lhsT_scale=t3s[:, j * 128 : (j + 1) * 128],
                    rhs=c4c[:].bitcast(FP8X4),
                    rhs_scale=c4s[:],
                    start=True,
                    stop=True,
                )
            pms.append(pm)
        new_codes(0)
        for n in range(SUB):
            quantise(0, n, n + 1)
        nc.scalar.copy(out=mAv[:, :, 0:4, :], in_=pms[0][:].rearrange("m j (x i) -> m x j i", i=4))
        nc.vector.tensor_copy(out=mAv[:, :, 4:8, :], in_=pms[1][:].rearrange("m j (x i) -> m x j i", i=4))

        transposes(1)
        for i in range(11, 13):
            load_x(i)
        mB = keep.tile([P, 1024], BF16, name="mB", align_bytes=64)
        mG = keep.tile([P, 1024], BF16, name="mG", align_bytes=64)
        mc = keep.tile([P, PASSES * OUT], U32, name="mc", align_bytes=64)
        ms = keep.tile([P, PASSES * OUT], U8, name="ms", align_bytes=64)
        nc.vector.transpose(out=mB[:], in_=mA[:])
        mGv = mG[:].rearrange("p (g a o t) -> p g a o t", g=2, a=16, o=8, t=4)
        mBv = mB[:].rearrange("p (t o g a) -> p g a o t", t=4, o=8, a=16, g=2)
        for g in range(2):
            nc.vector.tensor_copy(out=mGv[:, g], in_=mBv[:, g])
        nc.vector.quantize_mx(out=mc[:].bitcast(FP8X4), scales=ms[:], in_=mG[:])

        transposes(2)
        for i in range(13, 15):
            load_x(i)
        multiply(0)
        new_codes(1)
        quantise(1, 0, 2)
        quantise(1, 2, 4)
        reorder(3)

        transposes(3)
        load_x(15)
        new_codes(2)
        quantise(2, 0, 2)
        quantise(2, 2, 4)
        multiply(1)
        finish(0)
        multiply(2)
        finish(1)
        reorder(4)

        for i in range(4, NG - 1):
            transposes(i)
            new_codes(i - 1)
            quantise(i - 1, 0, 2)
            quantise(i - 1, 2, 4)
            multiply(i - 1)
            finish(i - 2)
            reorder(i + 1)

        last = NG - 1
        transposes(last)
        new_codes(last - 1)
        quantise(last - 1, 0, 2)
        finish(last - 2)
        quantise(last - 1, 2, 4)
        new_codes(last)
        quantise(last, 0, 1)
        quantise(last, 1, 2)
        multiply(last - 1)
        multiply(last, 0, 2)
        quantise(last, 2, 3)
        quantise(last, 3, 4)
        finish(last - 1)
        multiply(last, 2, 4)
        finish(last, 0, 2)
        finish(last, 2, 4)
